import numpy as np
import ml_dtypes


def mxq(x, axis, fmt="e4m3"):
    dtype, down = {"e4m3": (ml_dtypes.float8_e4m3fn, 7), "e5m2": (ml_dtypes.float8_e5m2, 14)}[fmt]
    v = np.moveaxis(np.asarray(x, np.float32).astype(ml_dtypes.bfloat16).astype(np.float64), axis, -1)
    blocks = v.reshape(v.shape[:-1] + (-1, 32))
    amax = np.abs(blocks).max(-1, keepdims=True)
    byte = np.maximum(np.where(amax > 0, np.frexp(amax)[1] - 1 + 127, 0) - down, 1)
    scale = np.exp2(byte - 127.0)
    codes = (blocks / scale).astype(np.float32).astype(dtype).astype(np.float64)
    return np.moveaxis((codes * scale).reshape(v.shape), -1, axis)


WIDE = False


def mx_kscale(k):
    if not WIDE:
        return np.ones(k)
    levels = np.array([10, -10, 5, -5, 0])
    a = np.random.permutation(np.resize(levels, k // 512 * 4)).reshape(k // 512, 4)
    idx = np.arange(k)
    return np.exp2(a[idx // 512, idx % 128 // 32])


BF16 = ml_dtypes.bfloat16


def bf(x):
    return np.asarray(x, np.float32).astype(BF16)


def f64(x):
    return np.asarray(x).astype(np.float64)


B, L, D, NC, DS = 2, 128, 1024, 2, 4
EPS = 2.0 ** -23


def rmsnorm(v, w):
    ms = np.mean(np.square(v), axis=-1, keepdims=True)
    return v * (1.0 / np.sqrt(ms + EPS)) * w


def setup_inputs():
    s = mx_kscale(D)
    s = s / s.max()
    t = mx_kscale(NC * D)
    tc = t.reshape(NC, D, 1)
    return {"x": bf(np.random.standard_normal((B, L, D)) * s),
            "W_in": bf(np.random.standard_normal((NC * D, D)) / np.sqrt(D) / s[None, :]),
            "W_out": bf(np.random.standard_normal((D, NC * D)) / np.sqrt(NC * D) / t[None, :]),
            "A_theta": bf(np.random.standard_normal((NC, D, DS)) * 0.5),
            "B_real": bf(np.random.standard_normal((NC, D, DS))),
            "B_imag": bf(np.random.standard_normal((NC, D, DS))),
            "C_real": bf(np.random.standard_normal((NC, D, DS)) / np.sqrt(2 * DS) * tc),
            "C_imag": bf(np.random.standard_normal((NC, D, DS)) / np.sqrt(2 * DS) * tc),
            "norm_w": bf(1.0 + 0.1 * np.random.standard_normal(D))}


def reference(x, W_in, W_out, A_theta, B_real, B_imag, C_real, C_imag, norm_w):
    x = f64(x)
    b, l, _ = x.shape
    xi = (mxq(x, 2, "e4m3") @ mxq(f64(W_in), 1, "e4m3").T).reshape(b, l, NC, D)[..., None]
    ct = np.cos(f64(A_theta))
    st = np.sin(f64(A_theta))
    rs = np.zeros((b, l, NC, D, DS))
    is_ = np.zeros_like(rs)
    bxr = f64(B_real) * xi
    bxi = f64(B_imag) * xi
    nr = ct * rs - st * is_ + bxr
    ni = st * rs + ct * is_ + bxi
    y = np.sum(f64(C_real) * nr - f64(C_imag) * ni, axis=-1)
    out = mxq(y.reshape(b, l, NC * D), 2, "e4m3") @ mxq(f64(W_out), 1, "e4m3").T
    return x + rmsnorm(out, f64(norm_w)), nr, ni

@@ -1,0 +1,439 @@
+from contextlib import ExitStack
+
+import concourse.mybir as mybir
+from concourse.masks import make_identity
+
+F32 = mybir.dt.float32
+BF16 = mybir.dt.bfloat16
+U32 = mybir.dt.uint32
+U8 = mybir.dt.uint8
+FP8X4 = mybir.dt.float8_e4m3fn_x4
+ALU = mybir.AluOpType
+ACT = mybir.ActivationFunctionType
+
+P = 128
+TOKENS = 256
+TOKEN_TILES = TOKENS // P
+D_MODEL = 1024
+FEATURES = 2048
+STATES = 4
+EPS = 2.0**-23
+
+K_PASS = 512
+PASS_WORDS = K_PASS // 2
+BANK = 512
+
+ROUNDS = 4
+CHUNK = FEATURES // ROUNDS
+IN_PASSES = D_MODEL // K_PASS
+OUT_PASSES = FEATURES // K_PASS
+OUT_COLS = D_MODEL // ROUNDS
+CHUNK_WORDS = 1024
+
+WEIGHT_CHUNKS = 2 * ROUNDS
+Y_OPERAND = WEIGHT_CHUNKS
+AHEAD = 3
+Y_ROUND = (Y_OPERAND - 1) // AHEAD
+
+GAIN_ROWS = FEATURES // (2 * P)
+TABLE_ROW = 2 * P
+TABLE_ROWS = FEATURES * STATES // TABLE_ROW
+
+FLOPS = 2 * TOKENS * D_MODEL * FEATURES * 2
+
+
+def tile_mamba3core_kernel(
+    tc, x, W_in, W_out, A_theta, B_real, B_imag, C_real, C_imag, norm_w, out_0, out_1, out_2
+):
+    nc = tc.nc
+    x_rows = x.flatten_outer_dims()
+    res_rows = out_0.flatten_outer_dims()
+    state_rows = [
+        out_1.rearrange("b l c d n -> (b l) (c d n)"),
+        out_2.rearrange("b l c d n -> (b l) (c d n)"),
+    ]
+    b_flat = [B_real.rearrange("c d n -> (c d n)"), B_imag.rearrange("c d n -> (c d n)")]
+    c_flat = [C_real.rearrange("c d n -> (c d n)"), C_imag.rearrange("c d n -> (c d n)")]
+
+    with ExitStack() as ctx:
+        keep = ctx.enter_context(tc.tile_pool(name="keep", bufs=1))
+        weights = ctx.enter_context(tc.tile_pool(name="weights", bufs=4))
+        grouping = ctx.enter_context(tc.tile_pool(name="grouping", bufs=3))
+        staging = ctx.enter_context(tc.tile_pool(name="staging", bufs=6))
+        y_rows = ctx.enter_context(tc.tile_pool(name="y_rows", bufs=2))
+        small = ctx.enter_context(tc.tile_pool(name="small", bufs=2))
+        xi_banks = ctx.enter_context(tc.psum_pool(name="xi_banks", bufs=4))
+        work_banks = ctx.enter_context(tc.psum_pool(name="work_banks", bufs=4))
+        ctx.enter_context(tc.manual_schedule())
+
+        ident = keep.tile([P, P], F32)
+        b_table = keep.tile([P, TABLE_ROW], BF16)
+        b_columns = keep.tile([P, P], F32)
+        b_real_all = keep.tile([P, FEATURES * STATES // 2], F32)
+        b_imag_all = keep.tile([P, FEATURES * STATES // 2], F32)
+        b_all = [b_real_all, b_imag_all]
+        b_rows = keep.tile([P, 2 * CHUNK_WORDS], BF16)
+        c_rows = keep.tile([P, 2 * CHUNK_WORDS], BF16)
+        gain_pad = keep.tile([P, 2 * P], F32)
+        gain = keep.tile([P, FEATURES // P], F32)
+        minus_half = keep.tile([P, 1], F32)
+        norm_w_all = keep.tile([P, D_MODEL], BF16)
+        x_sb = keep.tile([P, TOKEN_TILES * D_MODEL], BF16)
+        x_grouped = keep.tile([P, IN_PASSES * TOKENS, 2], F32, align_bytes=64)
+        y_grouped = keep.tile([P, OUT_PASSES * TOKENS * 4], BF16, align_bytes=64)
+        x_codes = keep.tile([P, IN_PASSES * TOKENS], U32, align_bytes=64)
+        x_scales = keep.tile([P, IN_PASSES * TOKENS], U8, align_bytes=64)
+        y_codes = keep.tile([P, OUT_PASSES * TOKENS], U32, align_bytes=64)
+        y_scales = keep.tile([P, OUT_PASSES * TOKENS], U8, align_bytes=64)
+        win_codes = keep.tile([P, ROUNDS, CHUNK_WORDS], U32, align_bytes=64)
+        win_scales = keep.tile([P, ROUNDS, CHUNK_WORDS], U8, align_bytes=64)
+        wout_codes = keep.tile([P, ROUNDS, CHUNK_WORDS], U32, align_bytes=64)
+        wout_scales = keep.tile([P, ROUNDS, CHUNK_WORDS], U8, align_bytes=64)
+
+        loaded = {}
+        grouped_of = {}
+        xi_of = {}
+        acc_of = {}
+
+        def load_weights(n):
+            w_sb = weights.tile([P, 4 * CHUNK_WORDS], BF16, tag="w_sb")
+            if n < ROUNDS:
+                nc.sync.dma_start(
+                    out=w_sb[:].rearrange("p (h e k) -> p h e k", h=2, e=2),
+                    in_=W_in[n * CHUNK : (n + 1) * CHUNK, :].rearrange(
+                        "(h p e) k -> p h e k", h=2, p=P, e=2
+                    ),
+                )
+            else:
+                first = (n - ROUNDS) * OUT_COLS
+                nc.sync.dma_start(
+                    out=w_sb[:].rearrange("p (i f) -> p i f", i=2),
+                    in_=W_out[first : first + OUT_COLS, :].rearrange("(i p) f -> p i f", p=P),
+                )
+            loaded[n] = w_sb
+
+        def k_to_partitions(rows_sb, row_tiles, passes, grouped):
+            words = rows_sb.bitcast(F32)
+            row_words = passes * PASS_WORDS
+            pairs = row_tiles // 2
+            for k_pass in range(passes):
+                for pair in range(pairs):
+                    bank = work_banks.tile([P, BANK], F32, tag="bank")
+                    for h in range(2):
+                        for s in range(2):
+                            first = (2 * pair + s) * row_words + k_pass * PASS_WORDS + h * P
+                            nc.tensor.transpose(
+                                out=bank[:, (2 * h + s) * P : (2 * h + s + 1) * P],
+                                in_=words[:, first : first + P],
+                                identity=ident[:],
+                            )
+                    column = (k_pass * pairs + pair) * 2 * P
+                    nc.scalar.copy(
+                        out=grouped[:, column : column + 2 * P, :],
+                        in_=bank[:].rearrange("p (h c) -> p c h", h=2),
+                    )
+
+        def prepare_weights(n):
+            grouped = grouping.tile([P, CHUNK_WORDS, 2], F32, tag="grouped", align_bytes=64)
+            passes = IN_PASSES if n < ROUNDS else OUT_PASSES
+            k_to_partitions(loaded[n][:], 8 // passes, passes, grouped)
+            grouped_of[n] = grouped[:].rearrange("p c h -> p (c h)").bitcast(BF16)
+            if n + ROUNDS < WEIGHT_CHUNKS:
+                load_weights(n + ROUNDS)
+
+        def quantise(n):
+            if n < ROUNDS:
+                codes, scales = win_codes[:, n, :], win_scales[:, n, :]
+            elif n < WEIGHT_CHUNKS:
+                codes, scales = wout_codes[:, n - ROUNDS, :], wout_scales[:, n - ROUNDS, :]
+            else:
+                codes, scales = y_codes[:], y_scales[:]
+            nc.vector.quantize_mx(out=codes.bitcast(FP8X4), scales=scales, in_=grouped_of[n])
+
+        def mx_pass(acc, a_codes, a_scales, b_codes, b_scales, first, last):
+            nc.tensor.matmul_mx(
+                out=acc,
+                lhsT=a_codes.bitcast(FP8X4),
+                lhsT_scale=a_scales,
+                rhs=b_codes.bitcast(FP8X4),
+                rhs_scale=b_scales,
+                start=first,
+                stop=last,
+            )
+
+        def spread_b(r, copy):
+            for part in range(2):
+                for h in range(2):
+                    block = 2 * r + h
+                    bank = work_banks.tile([P, BANK], F32, tag="bank")
+                    for i in range(4):
+                        row = part * TABLE_ROWS + 4 * block + i
+                        nc.tensor.transpose(
+                            out=bank[:, i * P : (i + 1) * P],
+                            in_=b_columns[:, row : row + 1].to_broadcast([P, P]),
+                            identity=ident[:],
+                        )
+                    copy(out=b_all[part][:, block * BANK : (block + 1) * BANK], in_=bank[:])
+
+        def xi_by_token(r):
+            for t in range(TOKEN_TILES):
+                xi = xi_banks.tile([P, CHUNK], F32, tag="xi")
+                for k_pass in range(IN_PASSES):
+                    toks = slice(k_pass * TOKENS + t * P, k_pass * TOKENS + (t + 1) * P)
+                    feats = slice(k_pass * CHUNK, (k_pass + 1) * CHUNK)
+                    mx_pass(
+                        xi[:],
+                        x_codes[:, toks],
+                        x_scales[:, toks],
+                        win_codes[:, r, feats],
+                        win_scales[:, r, feats],
+                        k_pass == 0,
+                        k_pass == IN_PASSES - 1,
+                    )
+                xi_of[(r, t)] = xi
+
+        def state_products(r, t, part):
+            prod = staging.tile([P, CHUNK * STATES], F32, tag="stage")
+            b_values = b_all[part][:].bitcast(BF16)
+            for h in range(2):
+                width = 2 * P * STATES
+                first = (2 * r + h) * width
+                xi_pairs = xi_of[(r, t)][:, h * 2 * P : (h + 1) * 2 * P].rearrange(
+                    "t (e q) -> t q e", e=2
+                )
+                nc.vector.tensor_tensor(
+                    out=prod[:, h * width : (h + 1) * width].rearrange(
+                        "t (q e n) -> t q e n", e=2, n=STATES
+                    ),
+                    in0=xi_pairs.unsqueeze(3).to_broadcast([P, P, 2, STATES]),
+                    in1=b_values[:, first : first + width].rearrange(
+                        "t (q e n) -> t q e n", e=2, n=STATES
+                    ),
+                    op=ALU.mult,
+                )
+            nc.sync.dma_start(
+                out=state_rows[part][
+                    t * P : (t + 1) * P, r * CHUNK * STATES : (r + 1) * CHUNK * STATES
+                ],
+                in_=prod[:],
+            )
+
+        def gain_in_rows():
+            rows = slice(0, GAIN_ROWS)
+            half = CHUNK_WORDS
+            products = staging.tile([P, CHUNK * STATES], F32, tag="stage")
+            sums = staging.tile([P, CHUNK * STATES], F32, tag="stage")
+            nc.gpsimd.tensor_tensor(
+                out=products[rows, :], in0=c_rows[rows, :], in1=b_rows[rows, :], op=ALU.mult
+            )
+            nc.gpsimd.tensor_tensor(
+                out=sums[rows, 0:half],
+                in0=products[rows, 0:half],
+                in1=products[rows, half : 2 * half],
+                op=ALU.subtract,
+            )
+            by_state = sums[rows, 0:half].rearrange("r (f n) -> r f n", n=STATES)
+            two_left = sums[rows, half : half + half // 2].rearrange("r (f n) -> r f n", n=2)
+            nc.gpsimd.tensor_tensor(
+                out=two_left, in0=by_state[:, :, 0:2], in1=by_state[:, :, 2:4], op=ALU.add
+            )
+            nc.gpsimd.tensor_tensor(
+                out=gain_pad[rows, :].rearrange("r (e q) -> r q e", e=2),
+                in0=two_left[:, :, 0].rearrange("r (q e) -> r q e", e=2),
+                in1=two_left[:, :, 1].rearrange("r (q e) -> r q e", e=2),
+                op=ALU.add,
+            )
+
+        def gain_to_partitions():
+            bank = work_banks.tile([P, BANK], F32, tag="bank")
+            for e in range(2):
+                nc.tensor.transpose(
+                    out=bank[:, e * P : (e + 1) * P],
+                    in_=gain_pad[:, e * P : (e + 1) * P],
+                    identity=ident[:],
+                )
+            nc.scalar.copy(
+                out=gain[:].rearrange("p (r e) -> p r e", e=2),
+                in_=bank[:, 0 : 2 * P].rearrange("p (e r) -> p r e", e=2)[:, 0:GAIN_ROWS, :],
+            )
+
+        def y_of_round(r):
+            y_lin = y_rows.tile([P, 4, TOKENS], BF16, tag="y_lin")
+            for pair in range(2):
+                bank = work_banks.tile([P, BANK], F32, tag="bank")
+                for s in range(2):
+                    j = 2 * pair + s
+                    for k_pass in range(IN_PASSES):
+                        feats = slice(k_pass * CHUNK + j * P, k_pass * CHUNK + (j + 1) * P)
+                        toks = slice(k_pass * TOKENS, (k_pass + 1) * TOKENS)
+                        mx_pass(
+                            bank[:, s * TOKENS : (s + 1) * TOKENS],
+                            win_codes[:, r, feats],
+                            win_scales[:, r, feats],
+                            x_codes[:, toks],
+                            x_scales[:, toks],
+                            k_pass == 0,
+                            k_pass == IN_PASSES - 1,
+                        )
+                for s in range(2):
+                    j = 2 * pair + s
+                    nc.scalar.activation(
+                        out=y_lin[:, j, :],
+                        in_=bank[:, s * TOKENS : (s + 1) * TOKENS],
+                        func=ACT.Copy,
+                        scale=gain[:, 4 * r + j : 4 * r + j + 1],
+                    )
+            nc.gpsimd.tensor_scalar(
+                out=y_grouped[:, r * 4 * TOKENS : (r + 1) * 4 * TOKENS].rearrange(
+                    "p (t j) -> p t j", j=4
+                ),
+                in0=y_lin[:].rearrange("p j t -> p t j"),
+                scalar1=1.0,
+                scalar2=0.0,
+                op0=ALU.mult,
+                op1=ALU.add,
+            )
+
+        def second_matmul():
+            for t in range(TOKEN_TILES):
+                for half in range(2):
+                    acc = work_banks.tile([P, BANK], F32, tag="bank")
+                    for s in range(2):
+                        chunk = 2 * half + s
+                        for k_pass in range(OUT_PASSES):
+                            toks = slice(k_pass * TOKENS + t * P, k_pass * TOKENS + (t + 1) * P)
+                            cols = slice(k_pass * OUT_COLS, (k_pass + 1) * OUT_COLS)
+                            mx_pass(
+                                acc[:, s * OUT_COLS : (s + 1) * OUT_COLS],
+                                y_codes[:, toks],
+                                y_scales[:, toks],
+                                wout_codes[:, chunk, cols],
+                                wout_scales[:, chunk, cols],
+                                k_pass == 0,
+                                k_pass == OUT_PASSES - 1,
+                            )
+                    acc_of[(t, half)] = acc
+
+        def norm_and_residual():
+            final_of = {}
+            rstd_of = {}
+            for t in range(TOKEN_TILES):
+                final = staging.tile([P, 2 * D_MODEL], F32, tag="stage")
+                sumsq = small.tile([P, 2], F32, tag="sumsq")
+                total = small.tile([P, 1], F32, tag="total")
+                mean_eps = small.tile([P, 1], F32, tag="mean_eps")
+                rstd = small.tile([P, 1], F32, tag="rstd")
+                for half in range(2):
+                    nc.scalar.activation(
+                        out=final[:, half * BANK : (half + 1) * BANK],
+                        in_=acc_of[(t, half)][:],
+                        func=ACT.Square,
+                        accum_out=sumsq[:, half : half + 1],
+                    )
+                nc.gpsimd.tensor_tensor(
+                    out=total[:], in0=sumsq[:, 0:1], in1=sumsq[:, 1:2], op=ALU.add
+                )
+                nc.gpsimd.tensor_scalar(
+                    out=mean_eps[:],
+                    in0=total[:],
+                    scalar1=1.0 / D_MODEL,
+                    scalar2=EPS,
+                    op0=ALU.mult,
+                    op1=ALU.add,
+                )
+                nc.gpsimd.tensor_tensor(
+                    out=rstd[:], in0=mean_eps[:], in1=minus_half[:], op=ALU.pow
+                )
+                final_of[t] = final
+                rstd_of[t] = rstd
+            for t in range(TOKEN_TILES):
+                final = final_of[t]
+                for half in range(2):
+                    nc.scalar.activation(
+                        out=final[:, half * BANK : (half + 1) * BANK],
+                        in_=acc_of[(t, half)][:],
+                        func=ACT.Copy,
+                        scale=rstd_of[t][:, 0:1],
+                    )
+                nc.gpsimd.tensor_tensor(
+                    out=final[:, D_MODEL : 2 * D_MODEL],
+                    in0=final[:, 0:D_MODEL],
+                    in1=norm_w_all[:],
+                    op=ALU.mult,
+                )
+                nc.gpsimd.tensor_tensor(
+                    out=final[:, 0:D_MODEL],
+                    in0=final[:, D_MODEL : 2 * D_MODEL],
+                    in1=x_sb[:, t * D_MODEL : (t + 1) * D_MODEL],
+                    op=ALU.add,
+                )
+                nc.scalar.dma_start(out=res_rows[t * P : (t + 1) * P, :], in_=final[:, 0:D_MODEL])
+
+        make_identity(nc, ident[:])
+        nc.gpsimd.memset(gain_pad[:], 0.0)
+        nc.gpsimd.memset(minus_half[:], -0.5)
+        nc.vector.memset(b_table[2 * TABLE_ROWS : P, :], 0.0)
+
+        for part in range(2):
+            nc.scalar.dma_start(
+                out=b_table[part * TABLE_ROWS : (part + 1) * TABLE_ROWS, :],
+                in_=b_flat[part].rearrange("(r w) -> r w", w=TABLE_ROW),
+            )
+        for part in range(2):
+            cols = slice(part * CHUNK_WORDS, (part + 1) * CHUNK_WORDS)
+            nc.scalar.dma_start(
+                out=b_rows[0:GAIN_ROWS, cols],
+                in_=b_flat[part].rearrange("(r w) -> r w", w=CHUNK_WORDS),
+            )
+            nc.scalar.dma_start(
+                out=c_rows[0:GAIN_ROWS, cols],
+                in_=c_flat[part].rearrange("(r w) -> r w", w=CHUNK_WORDS),
+            )
+        nc.sync.dma_start(
+            out=x_sb[:].rearrange("p (t k) -> p t k", t=TOKEN_TILES),
+            in_=x_rows.rearrange("(t p) k -> p t k", p=P),
+        )
+        for n in range(ROUNDS):
+            load_weights(n)
+
+        gain_in_rows()
+
+        bank = work_banks.tile([P, BANK], F32, tag="bank")
+        nc.tensor.transpose(out=bank[:, 0:P], in_=b_table[:].bitcast(F32), identity=ident[:])
+        nc.vector.tensor_copy(out=b_columns[:], in_=bank[:, 0:P])
+        spread_b(0, nc.vector.tensor_copy)
+
+        k_to_partitions(x_sb[:], TOKEN_TILES, IN_PASSES, x_grouped)
+        nc.vector.quantize_mx(
+            out=x_codes[:].bitcast(FP8X4),
+            scales=x_scales[:],
+            in_=x_grouped[:].rearrange("p c h -> p (c h)").bitcast(BF16),
+        )
+        prepare_weights(0)
+        quantise(0)
+        xi_by_token(0)
+        grouped_of[Y_OPERAND] = y_grouped[:]
+
+        for r in range(ROUNDS):
+            for n in range(AHEAD * r + 1, min(AHEAD * (r + 1), WEIGHT_CHUNKS - 1) + 1):
+                prepare_weights(n)
+            if r == 0:
+                nc.sync.dma_start(out=norm_w_all[:], in_=norm_w.partition_broadcast(P))
+            if r + 1 < ROUNDS:
+                spread_b(r + 1, nc.scalar.copy)
+            gap = 0
+            for t in range(TOKEN_TILES):
+                for part in range(2):
+                    state_products(r, t, part)
+                    gap += 1
+                    if gap <= AHEAD and AHEAD * r + gap <= Y_OPERAND:
+                        quantise(AHEAD * r + gap)
+            if r + 1 < ROUNDS:
+                xi_by_token(r + 1)
+            if r == 0:
+                gain_to_partitions()
+                for rr in range(ROUNDS):
+                    y_of_round(rr)
+            if r == Y_ROUND:
+                second_matmul()
+                norm_and_residual()

@@ -33,11 +33,12 @@ CHUNK_WORDS = 1024
 WEIGHT_CHUNKS = 2 * ROUNDS
 Y_OPERAND = WEIGHT_CHUNKS
 AHEAD = 3
-Y_ROUND = (Y_OPERAND - 1) // AHEAD
+SHARED_FROM = 2
 
 GAIN_ROWS = FEATURES // (2 * P)
 TABLE_ROW = 2 * P
 TABLE_ROWS = FEATURES * STATES // TABLE_ROW
+NORM_W_ROW = 2 * TABLE_ROWS
 
 FLOPS = 2 * TOKENS * D_MODEL * FEATURES * 2
 
@@ -59,16 +60,17 @@ def tile_mamba3core_kernel(
         keep = ctx.enter_context(tc.tile_pool(name="keep", bufs=1))
         weights = ctx.enter_context(tc.tile_pool(name="weights", bufs=4))
         grouping = ctx.enter_context(tc.tile_pool(name="grouping", bufs=3))
-        staging = ctx.enter_context(tc.tile_pool(name="staging", bufs=6))
+        staging = ctx.enter_context(tc.tile_pool(name="staging", bufs=7))
         y_rows = ctx.enter_context(tc.tile_pool(name="y_rows", bufs=2))
+        xi_copies = ctx.enter_context(tc.tile_pool(name="xi_copies", bufs=2))
         small = ctx.enter_context(tc.tile_pool(name="small", bufs=2))
         xi_banks = ctx.enter_context(tc.psum_pool(name="xi_banks", bufs=4))
         work_banks = ctx.enter_context(tc.psum_pool(name="work_banks", bufs=4))
         ctx.enter_context(tc.manual_schedule())
 
         ident = keep.tile([P, P], F32)
-        b_table = keep.tile([P, TABLE_ROW], BF16)
-        b_columns = keep.tile([P, P], F32)
+        table = keep.tile([P, TABLE_ROW], BF16)
+        table_columns = keep.tile([P, P], F32)
         b_real_all = keep.tile([P, FEATURES * STATES // 2], F32)
         b_imag_all = keep.tile([P, FEATURES * STATES // 2], F32)
         b_all = [b_real_all, b_imag_all]
@@ -77,7 +79,7 @@ def tile_mamba3core_kernel(
         gain_pad = keep.tile([P, 2 * P], F32)
         gain = keep.tile([P, FEATURES // P], F32)
         minus_half = keep.tile([P, 1], F32)
-        norm_w_all = keep.tile([P, D_MODEL], BF16)
+        norm_w_all = keep.tile([P, D_MODEL // 2], F32)
         x_sb = keep.tile([P, TOKEN_TILES * D_MODEL], BF16)
         x_grouped = keep.tile([P, IN_PASSES * TOKENS, 2], F32, align_bytes=64)
         y_grouped = keep.tile([P, OUT_PASSES * TOKENS * 4], BF16, align_bytes=64)
@@ -93,7 +95,10 @@ def tile_mamba3core_kernel(
         loaded = {}
         grouped_of = {}
         xi_of = {}
+        shared_of = {}
         acc_of = {}
+        rstd_of = {}
+        tiles_of_round = [(t, part) for t in range(TOKEN_TILES) for part in range(2)]
 
         def load_weights(n):
             w_sb = weights.tile([P, 4 * CHUNK_WORDS], BF16, tag="w_sb")
@@ -112,7 +117,7 @@ def tile_mamba3core_kernel(
                 )
             loaded[n] = w_sb
 
-        def k_to_partitions(rows_sb, row_tiles, passes, grouped):
+        def k_to_partitions(rows_sb, row_tiles, passes, grouped, copies):
             words = rows_sb.bitcast(F32)
             row_words = passes * PASS_WORDS
             pairs = row_tiles // 2
@@ -127,16 +132,17 @@ def tile_mamba3core_kernel(
                                 in_=words[:, first : first + P],
                                 identity=ident[:],
                             )
-                    column = (k_pass * pairs + pair) * 2 * P
-                    nc.scalar.copy(
+                    b = k_pass * pairs + pair
+                    column = b * 2 * P
+                    copies[b % len(copies)](
                         out=grouped[:, column : column + 2 * P, :],
                         in_=bank[:].rearrange("p (h c) -> p c h", h=2),
                     )
 
-        def prepare_weights(n):
+        def prepare_weights(n, copies):
             grouped = grouping.tile([P, CHUNK_WORDS, 2], F32, tag="grouped", align_bytes=64)
             passes = IN_PASSES if n < ROUNDS else OUT_PASSES
-            k_to_partitions(loaded[n][:], 8 // passes, passes, grouped)
+            k_to_partitions(loaded[n][:], 8 // passes, passes, grouped, copies)
             grouped_of[n] = grouped[:].rearrange("p c h -> p (c h)").bitcast(BF16)
             if n + ROUNDS < WEIGHT_CHUNKS:
                 load_weights(n + ROUNDS)
@@ -161,19 +167,26 @@ def tile_mamba3core_kernel(
                 stop=last,
             )
 
+        def spread_table_rows(first_row, dest, copy):
+            bank = work_banks.tile([P, BANK], F32, tag="bank")
+            for i in range(4):
+                row = first_row + i
+                nc.tensor.transpose(
+                    out=bank[:, i * P : (i + 1) * P],
+                    in_=table_columns[:, row : row + 1].to_broadcast([P, P]),
+                    identity=ident[:],
+                )
+            copy(out=dest, in_=bank[:])
+
         def spread_b(r, copy):
             for part in range(2):
                 for h in range(2):
                     block = 2 * r + h
-                    bank = work_banks.tile([P, BANK], F32, tag="bank")
-                    for i in range(4):
-                        row = part * TABLE_ROWS + 4 * block + i
-                        nc.tensor.transpose(
-                            out=bank[:, i * P : (i + 1) * P],
-                            in_=b_columns[:, row : row + 1].to_broadcast([P, P]),
-                            identity=ident[:],
-                        )
-                    copy(out=b_all[part][:, block * BANK : (block + 1) * BANK], in_=bank[:])
+                    spread_table_rows(
+                        part * TABLE_ROWS + 4 * block,
+                        b_all[part][:, block * BANK : (block + 1) * BANK],
+                        copy,
+                    )
 
         def xi_by_token(r):
             for t in range(TOKEN_TILES):
@@ -192,12 +205,37 @@ def tile_mamba3core_kernel(
                     )
                 xi_of[(r, t)] = xi
 
+        def b_values(r, h, part):
+            width = 2 * P * STATES
+            first = (2 * r + h) * width
+            return b_all[part][:].bitcast(BF16)[:, first : first + width]
+
+        def gpsimd_share(r):
+            xi_sb = xi_copies.tile([P, TOKEN_TILES, 2 * P], F32, tag="xi_sb")
+            for t in range(TOKEN_TILES):
+                nc.scalar.copy(
+                    out=xi_sb[:, t, :].rearrange("t (q e) -> t q e", e=2),
+                    in_=xi_of[(r, t)][:, 2 * P : 4 * P].rearrange("t (e q) -> t q e", e=2),
+                )
+            for t, part in tiles_of_round[1:]:
+                prod = staging.tile([P, CHUNK * STATES], F32, tag="stage")
+                nc.gpsimd.tensor_tensor(
+                    out=prod[:, CHUNK * STATES // 2 :].rearrange("t (f n) -> t f n", n=STATES),
+                    in0=xi_sb[:, t, :].unsqueeze(2).to_broadcast([P, 2 * P, STATES]),
+                    in1=b_values(r, 1, part).rearrange("t (f n) -> t f n", n=STATES),
+                    op=ALU.mult,
+                )
+                shared_of[(r, t, part)] = prod
+
         def state_products(r, t, part):
-            prod = staging.tile([P, CHUNK * STATES], F32, tag="stage")
-            b_values = b_all[part][:].bitcast(BF16)
-            for h in range(2):
-                width = 2 * P * STATES
-                first = (2 * r + h) * width
+            if (r, t, part) in shared_of:
+                prod = shared_of[(r, t, part)]
+                halves = [0]
+            else:
+                prod = staging.tile([P, CHUNK * STATES], F32, tag="stage")
+                halves = [0, 1]
+            width = 2 * P * STATES
+            for h in halves:
                 xi_pairs = xi_of[(r, t)][:, h * 2 * P : (h + 1) * 2 * P].rearrange(
                     "t (e q) -> t q e", e=2
                 )
@@ -206,9 +244,7 @@ def tile_mamba3core_kernel(
                         "t (q e n) -> t q e n", e=2, n=STATES
                     ),
                     in0=xi_pairs.unsqueeze(3).to_broadcast([P, P, 2, STATES]),
-                    in1=b_values[:, first : first + width].rearrange(
-                        "t (q e n) -> t q e n", e=2, n=STATES
-                    ),
+                    in1=b_values(r, h, part).rearrange("t (q e n) -> t q e n", e=2, n=STATES),
                     op=ALU.mult,
                 )
             nc.sync.dma_start(
@@ -314,18 +350,16 @@ def tile_mamba3core_kernel(
                             )
                     acc_of[(t, half)] = acc
 
-        def norm_and_residual():
-            final_of = {}
-            rstd_of = {}
+        def one_over_rms():
             for t in range(TOKEN_TILES):
-                final = staging.tile([P, 2 * D_MODEL], F32, tag="stage")
                 sumsq = small.tile([P, 2], F32, tag="sumsq")
                 total = small.tile([P, 1], F32, tag="total")
                 mean_eps = small.tile([P, 1], F32, tag="mean_eps")
                 rstd = small.tile([P, 1], F32, tag="rstd")
                 for half in range(2):
+                    unused = (2 * t + half) * BANK
                     nc.scalar.activation(
-                        out=final[:, half * BANK : (half + 1) * BANK],
+                        out=y_grouped[:, unused : unused + BANK],
                         in_=acc_of[(t, half)][:],
                         func=ACT.Square,
                         accum_out=sumsq[:, half : half + 1],
@@ -344,41 +378,57 @@ def tile_mamba3core_kernel(
                 nc.gpsimd.tensor_tensor(
                     out=rstd[:], in0=mean_eps[:], in1=minus_half[:], op=ALU.pow
                 )
-                final_of[t] = final
                 rstd_of[t] = rstd
-            for t in range(TOKEN_TILES):
-                final = final_of[t]
-                for half in range(2):
-                    nc.scalar.activation(
-                        out=final[:, half * BANK : (half + 1) * BANK],
-                        in_=acc_of[(t, half)][:],
-                        func=ACT.Copy,
-                        scale=rstd_of[t][:, 0:1],
-                    )
-                nc.gpsimd.tensor_tensor(
-                    out=final[:, D_MODEL : 2 * D_MODEL],
-                    in0=final[:, 0:D_MODEL],
-                    in1=norm_w_all[:],
-                    op=ALU.mult,
+
+        def finish_rows(t):
+            final = staging.tile([P, 2 * D_MODEL], F32, tag="stage")
+            norm_w_values = norm_w_all[:].bitcast(BF16)
+            for half in range(2):
+                cols = slice(half * BANK, (half + 1) * BANK)
+                nc.vector.scalar_tensor_tensor(
+                    out=final[:, cols],
+                    in0=acc_of[(t, half)][:],
+                    scalar=rstd_of[t][:, 0:1],
+                    in1=norm_w_values[:, cols],
+                    op0=ALU.mult,
+                    op1=ALU.mult,
                 )
-                nc.gpsimd.tensor_tensor(
-                    out=final[:, 0:D_MODEL],
-                    in0=final[:, D_MODEL : 2 * D_MODEL],
-                    in1=x_sb[:, t * D_MODEL : (t + 1) * D_MODEL],
-                    op=ALU.add,
-                )
-                nc.scalar.dma_start(out=res_rows[t * P : (t + 1) * P, :], in_=final[:, 0:D_MODEL])
+            nc.vector.tensor_tensor(
+                out=final[:, D_MODEL : 2 * D_MODEL],
+                in0=final[:, 0:D_MODEL],
+                in1=x_sb[:, t * D_MODEL : (t + 1) * D_MODEL],
+                op=ALU.add,
+            )
+            nc.scalar.dma_start(
+                out=res_rows[t * P : (t + 1) * P, :], in_=final[:, D_MODEL : 2 * D_MODEL]
+            )
+
+        def after_quantise(n):
+            if n + AHEAD < WEIGHT_CHUNKS:
+                prepare_weights(n + AHEAD, [nc.scalar.copy])
+            if n < ROUNDS:
+                y_of_round(n)
 
         make_identity(nc, ident[:])
         nc.gpsimd.memset(gain_pad[:], 0.0)
         nc.gpsimd.memset(minus_half[:], -0.5)
-        nc.vector.memset(b_table[2 * TABLE_ROWS : P, :], 0.0)
+        nc.vector.memset(table[NORM_W_ROW:P, :], 0.0)
 
         for part in range(2):
-            nc.scalar.dma_start(
-                out=b_table[part * TABLE_ROWS : (part + 1) * TABLE_ROWS, :],
+            nc.sync.dma_start(
+                out=table[part * TABLE_ROWS : (part + 1) * TABLE_ROWS, :],
                 in_=b_flat[part].rearrange("(r w) -> r w", w=TABLE_ROW),
             )
+        nc.sync.dma_start(
+            out=table[NORM_W_ROW : NORM_W_ROW + 4, :],
+            in_=norm_w.rearrange("(r w) -> r w", w=TABLE_ROW),
+        )
+        nc.sync.dma_start(
+            out=x_sb[:].rearrange("p (t k) -> p t k", t=TOKEN_TILES),
+            in_=x_rows.rearrange("(t p) k -> p t k", p=P),
+        )
+        for n in range(ROUNDS):
+            load_weights(n)
         for part in range(2):
             cols = slice(part * CHUNK_WORDS, (part + 1) * CHUNK_WORDS)
             nc.scalar.dma_start(
@@ -389,51 +439,51 @@ def tile_mamba3core_kernel(
                 out=c_rows[0:GAIN_ROWS, cols],
                 in_=c_flat[part].rearrange("(r w) -> r w", w=CHUNK_WORDS),
             )
-        nc.sync.dma_start(
-            out=x_sb[:].rearrange("p (t k) -> p t k", t=TOKEN_TILES),
-            in_=x_rows.rearrange("(t p) k -> p t k", p=P),
-        )
-        for n in range(ROUNDS):
-            load_weights(n)
 
         gain_in_rows()
 
+        both = [nc.scalar.copy, nc.vector.tensor_copy]
         bank = work_banks.tile([P, BANK], F32, tag="bank")
-        nc.tensor.transpose(out=bank[:, 0:P], in_=b_table[:].bitcast(F32), identity=ident[:])
-        nc.vector.tensor_copy(out=b_columns[:], in_=bank[:, 0:P])
+        nc.tensor.transpose(out=bank[:, 0:P], in_=table[:].bitcast(F32), identity=ident[:])
+        nc.vector.tensor_copy(out=table_columns[:], in_=bank[:, 0:P])
         spread_b(0, nc.vector.tensor_copy)
-
-        k_to_partitions(x_sb[:], TOKEN_TILES, IN_PASSES, x_grouped)
+        k_to_partitions(x_sb[:], TOKEN_TILES, IN_PASSES, x_grouped, both)
         nc.vector.quantize_mx(
             out=x_codes[:].bitcast(FP8X4),
             scales=x_scales[:],
             in_=x_grouped[:].rearrange("p c h -> p (c h)").bitcast(BF16),
         )
-        prepare_weights(0)
+        prepare_weights(0, both)
+        for n in range(1, AHEAD):
+            prepare_weights(n, [nc.scalar.copy])
         quantise(0)
         xi_by_token(0)
+        prepare_weights(AHEAD, [nc.scalar.copy])
+        gain_to_partitions()
+        y_of_round(0)
         grouped_of[Y_OPERAND] = y_grouped[:]
 
         for r in range(ROUNDS):
-            for n in range(AHEAD * r + 1, min(AHEAD * (r + 1), WEIGHT_CHUNKS - 1) + 1):
-                prepare_weights(n)
-            if r == 0:
-                nc.sync.dma_start(out=norm_w_all[:], in_=norm_w.partition_broadcast(P))
-            if r + 1 < ROUNDS:
-                spread_b(r + 1, nc.scalar.copy)
-            gap = 0
-            for t in range(TOKEN_TILES):
-                for part in range(2):
-                    state_products(r, t, part)
-                    gap += 1
-                    if gap <= AHEAD and AHEAD * r + gap <= Y_OPERAND:
-                        quantise(AHEAD * r + gap)
-            if r + 1 < ROUNDS:
-                xi_by_token(r + 1)
-            if r == 0:
-                gain_to_partitions()
-                for rr in range(ROUNDS):
-                    y_of_round(rr)
-            if r == Y_ROUND:
-                second_matmul()
-                norm_and_residual()
+            for i in range(len(tiles_of_round)):
+                t, part = tiles_of_round[i]
+                state_products(r, t, part)
+                n = r * len(tiles_of_round) + i + 1
+                if n < WEIGHT_CHUNKS:
+                    quantise(n)
+                    after_quantise(n)
+                if n == WEIGHT_CHUNKS - 1:
+                    quantise(Y_OPERAND)
+                    spread_table_rows(NORM_W_ROW, norm_w_all[:], nc.scalar.copy)
+                    second_matmul()
+                    one_over_rms()
+                if i == 0 and r + 1 < ROUNDS:
+                    xi_by_token(r + 1)
+                    if r == 0:
+                        spread_b(1, nc.scalar.copy)
+                    if r == 1:
+                        spread_b(2, nc.scalar.copy)
+                        spread_b(3, nc.scalar.copy)
+                    if r + 1 >= SHARED_FROM:
+                        gpsimd_share(r + 1)
+        for t in range(TOKEN_TILES):
+            finish_rows(t)

@@ -33,7 +33,7 @@ CHUNK_WORDS = 1024
 WEIGHT_CHUNKS = 2 * ROUNDS
 Y_OPERAND = WEIGHT_CHUNKS
 AHEAD = 3
-SHARED_FROM = 2
+SHARED_FROM = 1
 
 GAIN_ROWS = FEATURES // (2 * P)
 TABLE_ROW = 2 * P

@@ -32,8 +32,9 @@ CHUNK_WORDS = 1024
 
 WEIGHT_CHUNKS = 2 * ROUNDS
 Y_OPERAND = WEIGHT_CHUNKS
+RESIDENT = 6
+EARLY_CHUNKS = 4
 AHEAD = 3
-SHARED_FROM = 1
 
 GAIN_ROWS = FEATURES // (2 * P)
 TABLE_ROW = 2 * P
@@ -58,7 +59,7 @@ def tile_mamba3core_kernel(
 
     with ExitStack() as ctx:
         keep = ctx.enter_context(tc.tile_pool(name="keep", bufs=1))
-        weights = ctx.enter_context(tc.tile_pool(name="weights", bufs=4))
+        weights = ctx.enter_context(tc.tile_pool(name="weights", bufs=RESIDENT))
         grouping = ctx.enter_context(tc.tile_pool(name="grouping", bufs=3))
         staging = ctx.enter_context(tc.tile_pool(name="staging", bufs=7))
         y_rows = ctx.enter_context(tc.tile_pool(name="y_rows", bufs=2))
@@ -74,14 +75,13 @@ def tile_mamba3core_kernel(
         b_real_all = keep.tile([P, FEATURES * STATES // 2], F32)
         b_imag_all = keep.tile([P, FEATURES * STATES // 2], F32)
         b_all = [b_real_all, b_imag_all]
-        b_rows = keep.tile([P, 2 * CHUNK_WORDS], BF16)
-        c_rows = keep.tile([P, 2 * CHUNK_WORDS], BF16)
         gain_pad = keep.tile([P, 2 * P], F32)
         gain = keep.tile([P, FEATURES // P], F32)
-        minus_half = keep.tile([P, 1], F32)
+        one = keep.tile([P, 1], F32)
+        warm = keep.tile([P, 1], F32)
+        eps_column = keep.tile([P, 1], F32)
         norm_w_all = keep.tile([P, D_MODEL // 2], F32)
         x_sb = keep.tile([P, TOKEN_TILES * D_MODEL], BF16)
-        x_grouped = keep.tile([P, IN_PASSES * TOKENS, 2], F32, align_bytes=64)
         y_grouped = keep.tile([P, OUT_PASSES * TOKENS * 4], BF16, align_bytes=64)
         x_codes = keep.tile([P, IN_PASSES * TOKENS], U32, align_bytes=64)
         x_scales = keep.tile([P, IN_PASSES * TOKENS], U8, align_bytes=64)
@@ -95,6 +95,7 @@ def tile_mamba3core_kernel(
         loaded = {}
         grouped_of = {}
         xi_of = {}
+        xi_sb_of = {}
         shared_of = {}
         acc_of = {}
         rstd_of = {}
@@ -103,12 +104,15 @@ def tile_mamba3core_kernel(
         def load_weights(n):
             w_sb = weights.tile([P, 4 * CHUNK_WORDS], BF16, tag="w_sb")
             if n < ROUNDS:
-                nc.sync.dma_start(
-                    out=w_sb[:].rearrange("p (h e k) -> p h e k", h=2, e=2),
-                    in_=W_in[n * CHUNK : (n + 1) * CHUNK, :].rearrange(
-                        "(h p e) k -> p h e k", h=2, p=P, e=2
-                    ),
+                sbuf_side = w_sb[:].rearrange("p (h e k) -> p h e k", h=2, e=2)
+                dram_side = W_in[n * CHUNK : (n + 1) * CHUNK, :].rearrange(
+                    "(h p e) k -> p h e k", h=2, p=P, e=2
                 )
+                if n == 0:
+                    for h in range(2):
+                        nc.sync.dma_start(out=sbuf_side[:, h], in_=dram_side[:, h])
+                else:
+                    nc.sync.dma_start(out=sbuf_side, in_=dram_side)
             else:
                 first = (n - ROUNDS) * OUT_COLS
                 nc.sync.dma_start(
@@ -121,8 +125,8 @@ def tile_mamba3core_kernel(
             words = rows_sb.bitcast(F32)
             row_words = passes * PASS_WORDS
             pairs = row_tiles // 2
-            for k_pass in range(passes):
-                for pair in range(pairs):
+            for pair in range(pairs):
+                for k_pass in range(passes):
                     bank = work_banks.tile([P, BANK], F32, tag="bank")
                     for h in range(2):
                         for s in range(2):
@@ -132,9 +136,8 @@ def tile_mamba3core_kernel(
                                 in_=words[:, first : first + P],
                                 identity=ident[:],
                             )
-                    b = k_pass * pairs + pair
-                    column = b * 2 * P
-                    copies[b % len(copies)](
+                    column = (k_pass * pairs + pair) * 2 * P
+                    copies[k_pass % len(copies)](
                         out=grouped[:, column : column + 2 * P, :],
                         in_=bank[:].rearrange("p (h c) -> p c h", h=2),
                     )
@@ -144,8 +147,8 @@ def tile_mamba3core_kernel(
             passes = IN_PASSES if n < ROUNDS else OUT_PASSES
             k_to_partitions(loaded[n][:], 8 // passes, passes, grouped, copies)
             grouped_of[n] = grouped[:].rearrange("p c h -> p (c h)").bitcast(BF16)
-            if n + ROUNDS < WEIGHT_CHUNKS:
-                load_weights(n + ROUNDS)
+            if n + RESIDENT < WEIGHT_CHUNKS:
+                load_weights(n + RESIDENT)
 
         def quantise(n):
             if n < ROUNDS:
@@ -210,18 +213,21 @@ def tile_mamba3core_kernel(
             first = (2 * r + h) * width
             return b_all[part][:].bitcast(BF16)[:, first : first + width]
 
-        def gpsimd_share(r):
+        def xi_for_gpsimd(r):
             xi_sb = xi_copies.tile([P, TOKEN_TILES, 2 * P], F32, tag="xi_sb")
             for t in range(TOKEN_TILES):
                 nc.scalar.copy(
                     out=xi_sb[:, t, :].rearrange("t (q e) -> t q e", e=2),
                     in_=xi_of[(r, t)][:, 2 * P : 4 * P].rearrange("t (e q) -> t q e", e=2),
                 )
+            xi_sb_of[r] = xi_sb
+
+        def gpsimd_share(r):
             for t, part in tiles_of_round[1:]:
                 prod = staging.tile([P, CHUNK * STATES], F32, tag="stage")
                 nc.gpsimd.tensor_tensor(
                     out=prod[:, CHUNK * STATES // 2 :].rearrange("t (f n) -> t f n", n=STATES),
-                    in0=xi_sb[:, t, :].unsqueeze(2).to_broadcast([P, 2 * P, STATES]),
+                    in0=xi_sb_of[r][:, t, :].unsqueeze(2).to_broadcast([P, 2 * P, STATES]),
                     in1=b_values(r, 1, part).rearrange("t (f n) -> t f n", n=STATES),
                     op=ALU.mult,
                 )
@@ -257,6 +263,17 @@ def tile_mamba3core_kernel(
         def gain_in_rows():
             rows = slice(0, GAIN_ROWS)
             half = CHUNK_WORDS
+            inputs = staging.tile([P, CHUNK * STATES], F32, tag="stage")
+            b_rows = inputs[:].bitcast(BF16)[:, 0 : 2 * half]
+            c_rows = inputs[:].bitcast(BF16)[:, 2 * half : 4 * half]
+            for part in range(2):
+                cols = slice(part * half, (part + 1) * half)
+                nc.scalar.dma_start(
+                    out=b_rows[rows, cols], in_=b_flat[part].rearrange("(r w) -> r w", w=half)
+                )
+                nc.scalar.dma_start(
+                    out=c_rows[rows, cols], in_=c_flat[part].rearrange("(r w) -> r w", w=half)
+                )
             products = staging.tile([P, CHUNK * STATES], F32, tag="stage")
             sums = staging.tile([P, CHUNK * STATES], F32, tag="stage")
             nc.gpsimd.tensor_tensor(
@@ -352,9 +369,8 @@ def tile_mamba3core_kernel(
 
         def one_over_rms():
             for t in range(TOKEN_TILES):
-                sumsq = small.tile([P, 2], F32, tag="sumsq")
-                total = small.tile([P, 1], F32, tag="total")
-                mean_eps = small.tile([P, 1], F32, tag="mean_eps")
+                mean_sq = small.tile([P, 2], F32, tag="mean_sq")
+                rest = small.tile([P, 1], F32, tag="rest")
                 rstd = small.tile([P, 1], F32, tag="rstd")
                 for half in range(2):
                     unused = (2 * t + half) * BANK
@@ -362,21 +378,17 @@ def tile_mamba3core_kernel(
                         out=y_grouped[:, unused : unused + BANK],
                         in_=acc_of[(t, half)][:],
                         func=ACT.Square,
-                        accum_out=sumsq[:, half : half + 1],
+                        scale=D_MODEL**-0.5,
+                        accum_out=mean_sq[:, half : half + 1],
                     )
-                nc.gpsimd.tensor_tensor(
-                    out=total[:], in0=sumsq[:, 0:1], in1=sumsq[:, 1:2], op=ALU.add
+                nc.scalar.activation(
+                    out=rest[:], in_=mean_sq[:, 1:2], func=ACT.Identity, bias=eps_column[:, 0:1]
                 )
-                nc.gpsimd.tensor_scalar(
-                    out=mean_eps[:],
-                    in0=total[:],
-                    scalar1=1.0 / D_MODEL,
-                    scalar2=EPS,
-                    op0=ALU.mult,
-                    op1=ALU.add,
-                )
-                nc.gpsimd.tensor_tensor(
-                    out=rstd[:], in0=mean_eps[:], in1=minus_half[:], op=ALU.pow
+                nc.scalar.activation(
+                    out=rstd[:],
+                    in_=mean_sq[:, 0:1],
+                    func=ACT.Abs_reciprocal_sqrt,
+                    bias=rest[:, 0:1],
                 )
                 rstd_of[t] = rstd
 
@@ -411,7 +423,8 @@ def tile_mamba3core_kernel(
 
         make_identity(nc, ident[:])
         nc.gpsimd.memset(gain_pad[:], 0.0)
-        nc.gpsimd.memset(minus_half[:], -0.5)
+        nc.gpsimd.memset(one[:], 1.0)
+        nc.gpsimd.memset(eps_column[:], EPS)
         nc.vector.memset(table[NORM_W_ROW:P, :], 0.0)
 
         for part in range(2):
@@ -427,38 +440,31 @@ def tile_mamba3core_kernel(
             out=x_sb[:].rearrange("p (t k) -> p t k", t=TOKEN_TILES),
             in_=x_rows.rearrange("(t p) k -> p t k", p=P),
         )
-        for n in range(ROUNDS):
+        for n in range(RESIDENT):
             load_weights(n)
-        for part in range(2):
-            cols = slice(part * CHUNK_WORDS, (part + 1) * CHUNK_WORDS)
-            nc.scalar.dma_start(
-                out=b_rows[0:GAIN_ROWS, cols],
-                in_=b_flat[part].rearrange("(r w) -> r w", w=CHUNK_WORDS),
-            )
-            nc.scalar.dma_start(
-                out=c_rows[0:GAIN_ROWS, cols],
-                in_=c_flat[part].rearrange("(r w) -> r w", w=CHUNK_WORDS),
-            )
 
         gain_in_rows()
+
+        nc.scalar.activation(out=warm[:], in_=one[:], func=ACT.Abs_reciprocal_sqrt)
 
         both = [nc.scalar.copy, nc.vector.tensor_copy]
         bank = work_banks.tile([P, BANK], F32, tag="bank")
         nc.tensor.transpose(out=bank[:, 0:P], in_=table[:].bitcast(F32), identity=ident[:])
         nc.vector.tensor_copy(out=table_columns[:], in_=bank[:, 0:P])
-        spread_b(0, nc.vector.tensor_copy)
+        x_grouped = grouping.tile([P, CHUNK_WORDS, 2], F32, tag="grouped", align_bytes=64)
+        x_columns = IN_PASSES * TOKENS
         k_to_partitions(x_sb[:], TOKEN_TILES, IN_PASSES, x_grouped, both)
         nc.vector.quantize_mx(
             out=x_codes[:].bitcast(FP8X4),
             scales=x_scales[:],
-            in_=x_grouped[:].rearrange("p c h -> p (c h)").bitcast(BF16),
+            in_=x_grouped[:, 0:x_columns, :].rearrange("p c h -> p (c h)").bitcast(BF16),
         )
         prepare_weights(0, both)
-        for n in range(1, AHEAD):
-            prepare_weights(n, [nc.scalar.copy])
+        spread_b(0, nc.scalar.copy)
         quantise(0)
         xi_by_token(0)
-        prepare_weights(AHEAD, [nc.scalar.copy])
+        for n in range(1, AHEAD + 1):
+            prepare_weights(n, [nc.scalar.copy])
         gain_to_partitions()
         y_of_round(0)
         grouped_of[Y_OPERAND] = y_grouped[:]
@@ -467,23 +473,33 @@ def tile_mamba3core_kernel(
             for i in range(len(tiles_of_round)):
                 t, part = tiles_of_round[i]
                 state_products(r, t, part)
-                n = r * len(tiles_of_round) + i + 1
+                done = r * len(tiles_of_round) + i + 1
+                if done <= EARLY_CHUNKS:
+                    n = done
+                elif done % 2 == 0:
+                    n = EARLY_CHUNKS + (done - EARLY_CHUNKS) // 2
+                else:
+                    n = WEIGHT_CHUNKS
                 if n < WEIGHT_CHUNKS:
                     quantise(n)
+                if n == 1:
+                    xi_by_token(1)
+                    spread_b(1, nc.scalar.copy)
+                if n < WEIGHT_CHUNKS:
                     after_quantise(n)
+                if n == WEIGHT_CHUNKS - AHEAD:
+                    spread_b(2, nc.scalar.copy)
+                    gpsimd_share(2)
+                    spread_b(3, nc.scalar.copy)
+                    spread_table_rows(NORM_W_ROW, norm_w_all[:], nc.scalar.copy)
+                if r == 2 and i == 0:
+                    gpsimd_share(3)
                 if n == WEIGHT_CHUNKS - 1:
                     quantise(Y_OPERAND)
-                    spread_table_rows(NORM_W_ROW, norm_w_all[:], nc.scalar.copy)
                     second_matmul()
                     one_over_rms()
-                if i == 0 and r + 1 < ROUNDS:
-                    xi_by_token(r + 1)
-                    if r == 0:
-                        spread_b(1, nc.scalar.copy)
-                    if r == 1:
-                        spread_b(2, nc.scalar.copy)
-                        spread_b(3, nc.scalar.copy)
-                    if r + 1 >= SHARED_FROM:
-                        gpsimd_share(r + 1)
+            if r + 2 < ROUNDS:
+                xi_by_token(r + 2)
+                xi_for_gpsimd(r + 2)
         for t in range(TOKEN_TILES):
             finish_rows(t)

from contextlib import ExitStack

import concourse.mybir as mybir
from concourse.masks import make_identity

F32 = mybir.dt.float32
BF16 = mybir.dt.bfloat16
U32 = mybir.dt.uint32
U8 = mybir.dt.uint8
FP8X4 = mybir.dt.float8_e4m3fn_x4
ALU = mybir.AluOpType
ACT = mybir.ActivationFunctionType

P = 128
TOKENS = 256
TOKEN_TILES = TOKENS // P
D_MODEL = 1024
FEATURES = 2048
STATES = 4
EPS = 2.0**-23

K_PASS = 512
PASS_WORDS = K_PASS // 2
BANK = 512

ROUNDS = 4
CHUNK = FEATURES // ROUNDS
IN_PASSES = D_MODEL // K_PASS
OUT_PASSES = FEATURES // K_PASS
OUT_COLS = D_MODEL // ROUNDS
CHUNK_WORDS = 1024

WEIGHT_CHUNKS = 2 * ROUNDS
Y_OPERAND = WEIGHT_CHUNKS
RESIDENT = 6
EARLY_CHUNKS = 4
AHEAD = 3

GAIN_ROWS = FEATURES // (2 * P)
TABLE_ROW = 2 * P
TABLE_ROWS = FEATURES * STATES // TABLE_ROW
NORM_W_ROW = 2 * TABLE_ROWS

FLOPS = 2 * TOKENS * D_MODEL * FEATURES * 2


def tile_mamba3core_kernel(
    tc, x, W_in, W_out, A_theta, B_real, B_imag, C_real, C_imag, norm_w, out_0, out_1, out_2
):
    nc = tc.nc
    x_rows = x.flatten_outer_dims()
    res_rows = out_0.flatten_outer_dims()
    state_rows = [
        out_1.rearrange("b l c d n -> (b l) (c d n)"),
        out_2.rearrange("b l c d n -> (b l) (c d n)"),
    ]
    b_flat = [B_real.rearrange("c d n -> (c d n)"), B_imag.rearrange("c d n -> (c d n)")]
    c_flat = [C_real.rearrange("c d n -> (c d n)"), C_imag.rearrange("c d n -> (c d n)")]

    with ExitStack() as ctx:
        keep = ctx.enter_context(tc.tile_pool(name="keep", bufs=1))
        weights = ctx.enter_context(tc.tile_pool(name="weights", bufs=RESIDENT))
        grouping = ctx.enter_context(tc.tile_pool(name="grouping", bufs=3))
        staging = ctx.enter_context(tc.tile_pool(name="staging", bufs=7))
        y_rows = ctx.enter_context(tc.tile_pool(name="y_rows", bufs=2))
        xi_copies = ctx.enter_context(tc.tile_pool(name="xi_copies", bufs=2))
        small = ctx.enter_context(tc.tile_pool(name="small", bufs=2))
        xi_banks = ctx.enter_context(tc.psum_pool(name="xi_banks", bufs=4))
        work_banks = ctx.enter_context(tc.psum_pool(name="work_banks", bufs=4))
        ctx.enter_context(tc.manual_schedule())

        ident = keep.tile([P, P], F32)
        table = keep.tile([P, TABLE_ROW], BF16)
        table_columns = keep.tile([P, P], F32)
        b_real_all = keep.tile([P, FEATURES * STATES // 2], F32)
        b_imag_all = keep.tile([P, FEATURES * STATES // 2], F32)
        b_all = [b_real_all, b_imag_all]
        gain_pad = keep.tile([P, 2 * P], F32)
        gain = keep.tile([P, FEATURES // P], F32)
        one = keep.tile([P, 1], F32)
        warm = keep.tile([P, 1], F32)
        eps_column = keep.tile([P, 1], F32)
        norm_w_all = keep.tile([P, D_MODEL // 2], F32)
        x_sb = keep.tile([P, TOKEN_TILES * D_MODEL], BF16)
        y_grouped = keep.tile([P, OUT_PASSES * TOKENS * 4], BF16, align_bytes=64)
        x_codes = keep.tile([P, IN_PASSES * TOKENS], U32, align_bytes=64)
        x_scales = keep.tile([P, IN_PASSES * TOKENS], U8, align_bytes=64)
        y_codes = keep.tile([P, OUT_PASSES * TOKENS], U32, align_bytes=64)
        y_scales = keep.tile([P, OUT_PASSES * TOKENS], U8, align_bytes=64)
        win_codes = keep.tile([P, ROUNDS, CHUNK_WORDS], U32, align_bytes=64)
        win_scales = keep.tile([P, ROUNDS, CHUNK_WORDS], U8, align_bytes=64)
        wout_codes = keep.tile([P, ROUNDS, CHUNK_WORDS], U32, align_bytes=64)
        wout_scales = keep.tile([P, ROUNDS, CHUNK_WORDS], U8, align_bytes=64)

        loaded = {}
        grouped_of = {}
        xi_of = {}
        xi_sb_of = {}
        shared_of = {}
        acc_of = {}
        rstd_of = {}
        tiles_of_round = [(t, part) for t in range(TOKEN_TILES) for part in range(2)]

        def load_weights(n):
            w_sb = weights.tile([P, 4 * CHUNK_WORDS], BF16, tag="w_sb")
            if n < ROUNDS:
                sbuf_side = w_sb[:].rearrange("p (h e k) -> p h e k", h=2, e=2)
                dram_side = W_in[n * CHUNK : (n + 1) * CHUNK, :].rearrange(
                    "(h p e) k -> p h e k", h=2, p=P, e=2
                )
                if n == 0:
                    for h in range(2):
                        nc.sync.dma_start(out=sbuf_side[:, h], in_=dram_side[:, h])
                else:
                    nc.sync.dma_start(out=sbuf_side, in_=dram_side)
            else:
                first = (n - ROUNDS) * OUT_COLS
                nc.sync.dma_start(
                    out=w_sb[:].rearrange("p (i f) -> p i f", i=2),
                    in_=W_out[first : first + OUT_COLS, :].rearrange("(i p) f -> p i f", p=P),
                )
            loaded[n] = w_sb

        def k_to_partitions(rows_sb, row_tiles, passes, grouped, copies):
            words = rows_sb.bitcast(F32)
            row_words = passes * PASS_WORDS
            pairs = row_tiles // 2
            for pair in range(pairs):
                for k_pass in range(passes):
                    bank = work_banks.tile([P, BANK], F32, tag="bank")
                    for h in range(2):
                        for s in range(2):
                            first = (2 * pair + s) * row_words + k_pass * PASS_WORDS + h * P
                            nc.tensor.transpose(
                                out=bank[:, (2 * h + s) * P : (2 * h + s + 1) * P],
                                in_=words[:, first : first + P],
                                identity=ident[:],
                            )
                    column = (k_pass * pairs + pair) * 2 * P
                    copies[k_pass % len(copies)](
                        out=grouped[:, column : column + 2 * P, :],
                        in_=bank[:].rearrange("p (h c) -> p c h", h=2),
                    )

        def prepare_weights(n, copies):
            grouped = grouping.tile([P, CHUNK_WORDS, 2], F32, tag="grouped", align_bytes=64)
            passes = IN_PASSES if n < ROUNDS else OUT_PASSES
            k_to_partitions(loaded[n][:], 8 // passes, passes, grouped, copies)
            grouped_of[n] = grouped[:].rearrange("p c h -> p (c h)").bitcast(BF16)
            if n + RESIDENT < WEIGHT_CHUNKS:
                load_weights(n + RESIDENT)

        def quantise(n):
            if n < ROUNDS:
                codes, scales = win_codes[:, n, :], win_scales[:, n, :]
            elif n < WEIGHT_CHUNKS:
                codes, scales = wout_codes[:, n - ROUNDS, :], wout_scales[:, n - ROUNDS, :]
            else:
                codes, scales = y_codes[:], y_scales[:]
            nc.vector.quantize_mx(out=codes.bitcast(FP8X4), scales=scales, in_=grouped_of[n])

        def mx_pass(acc, a_codes, a_scales, b_codes, b_scales, first, last):
            nc.tensor.matmul_mx(
                out=acc,
                lhsT=a_codes.bitcast(FP8X4),
                lhsT_scale=a_scales,
                rhs=b_codes.bitcast(FP8X4),
                rhs_scale=b_scales,
                start=first,
                stop=last,
            )

        def spread_table_rows(first_row, dest, copy):
            bank = work_banks.tile([P, BANK], F32, tag="bank")
            for i in range(4):
                row = first_row + i
                nc.tensor.transpose(
                    out=bank[:, i * P : (i + 1) * P],
                    in_=table_columns[:, row : row + 1].to_broadcast([P, P]),
                    identity=ident[:],
                )
            copy(out=dest, in_=bank[:])

        def spread_b(r, copy):
            for part in range(2):
                for h in range(2):
                    block = 2 * r + h
                    spread_table_rows(
                        part * TABLE_ROWS + 4 * block,
                        b_all[part][:, block * BANK : (block + 1) * BANK],
                        copy,
                    )

        def xi_by_token(r):
            for t in range(TOKEN_TILES):
                xi = xi_banks.tile([P, CHUNK], F32, tag="xi")
                for k_pass in range(IN_PASSES):
                    toks = slice(k_pass * TOKENS + t * P, k_pass * TOKENS + (t + 1) * P)
                    feats = slice(k_pass * CHUNK, (k_pass + 1) * CHUNK)
                    mx_pass(
                        xi[:],
                        x_codes[:, toks],
                        x_scales[:, toks],
                        win_codes[:, r, feats],
                        win_scales[:, r, feats],
                        k_pass == 0,
                        k_pass == IN_PASSES - 1,
                    )
                xi_of[(r, t)] = xi

        def b_values(r, h, part):
            width = 2 * P * STATES
            first = (2 * r + h) * width
            return b_all[part][:].bitcast(BF16)[:, first : first + width]

        def xi_for_gpsimd(r):
            xi_sb = xi_copies.tile([P, TOKEN_TILES, 2 * P], F32, tag="xi_sb")
            for t in range(TOKEN_TILES):
                nc.scalar.copy(
                    out=xi_sb[:, t, :].rearrange("t (q e) -> t q e", e=2),
                    in_=xi_of[(r, t)][:, 2 * P : 4 * P].rearrange("t (e q) -> t q e", e=2),
                )
            xi_sb_of[r] = xi_sb

        def gpsimd_share(r):
            for t, part in tiles_of_round[1:]:
                prod = staging.tile([P, CHUNK * STATES], F32, tag="stage")
                nc.gpsimd.tensor_tensor(
                    out=prod[:, CHUNK * STATES // 2 :].rearrange("t (f n) -> t f n", n=STATES),
                    in0=xi_sb_of[r][:, t, :].unsqueeze(2).to_broadcast([P, 2 * P, STATES]),
                    in1=b_values(r, 1, part).rearrange("t (f n) -> t f n", n=STATES),
                    op=ALU.mult,
                )
                shared_of[(r, t, part)] = prod

        def state_products(r, t, part):
            if (r, t, part) in shared_of:
                prod = shared_of[(r, t, part)]
                halves = [0]
            else:
                prod = staging.tile([P, CHUNK * STATES], F32, tag="stage")
                halves = [0, 1]
            width = 2 * P * STATES
            for h in halves:
                xi_pairs = xi_of[(r, t)][:, h * 2 * P : (h + 1) * 2 * P].rearrange(
                    "t (e q) -> t q e", e=2
                )
                nc.vector.tensor_tensor(
                    out=prod[:, h * width : (h + 1) * width].rearrange(
                        "t (q e n) -> t q e n", e=2, n=STATES
                    ),
                    in0=xi_pairs.unsqueeze(3).to_broadcast([P, P, 2, STATES]),
                    in1=b_values(r, h, part).rearrange("t (q e n) -> t q e n", e=2, n=STATES),
                    op=ALU.mult,
                )
            nc.sync.dma_start(
                out=state_rows[part][
                    t * P : (t + 1) * P, r * CHUNK * STATES : (r + 1) * CHUNK * STATES
                ],
                in_=prod[:],
            )

        def gain_in_rows():
            rows = slice(0, GAIN_ROWS)
            half = CHUNK_WORDS
            inputs = staging.tile([P, CHUNK * STATES], F32, tag="stage")
            b_rows = inputs[:].bitcast(BF16)[:, 0 : 2 * half]
            c_rows = inputs[:].bitcast(BF16)[:, 2 * half : 4 * half]
            for part in range(2):
                cols = slice(part * half, (part + 1) * half)
                nc.scalar.dma_start(
                    out=b_rows[rows, cols], in_=b_flat[part].rearrange("(r w) -> r w", w=half)
                )
                nc.scalar.dma_start(
                    out=c_rows[rows, cols], in_=c_flat[part].rearrange("(r w) -> r w", w=half)
                )
            products = staging.tile([P, CHUNK * STATES], F32, tag="stage")
            sums = staging.tile([P, CHUNK * STATES], F32, tag="stage")
            nc.gpsimd.tensor_tensor(
                out=products[rows, :], in0=c_rows[rows, :], in1=b_rows[rows, :], op=ALU.mult
            )
            nc.gpsimd.tensor_tensor(
                out=sums[rows, 0:half],
                in0=products[rows, 0:half],
                in1=products[rows, half : 2 * half],
                op=ALU.subtract,
            )
            by_state = sums[rows, 0:half].rearrange("r (f n) -> r f n", n=STATES)
            two_left = sums[rows, half : half + half // 2].rearrange("r (f n) -> r f n", n=2)
            nc.gpsimd.tensor_tensor(
                out=two_left, in0=by_state[:, :, 0:2], in1=by_state[:, :, 2:4], op=ALU.add
            )
            nc.gpsimd.tensor_tensor(
                out=gain_pad[rows, :].rearrange("r (e q) -> r q e", e=2),
                in0=two_left[:, :, 0].rearrange("r (q e) -> r q e", e=2),
                in1=two_left[:, :, 1].rearrange("r (q e) -> r q e", e=2),
                op=ALU.add,
            )

        def gain_to_partitions():
            bank = work_banks.tile([P, BANK], F32, tag="bank")
            for e in range(2):
                nc.tensor.transpose(
                    out=bank[:, e * P : (e + 1) * P],
                    in_=gain_pad[:, e * P : (e + 1) * P],
                    identity=ident[:],
                )
            nc.scalar.copy(
                out=gain[:].rearrange("p (r e) -> p r e", e=2),
                in_=bank[:, 0 : 2 * P].rearrange("p (e r) -> p r e", e=2)[:, 0:GAIN_ROWS, :],
            )

        def y_of_round(r):
            y_lin = y_rows.tile([P, 4, TOKENS], BF16, tag="y_lin")
            for pair in range(2):
                bank = work_banks.tile([P, BANK], F32, tag="bank")
                for s in range(2):
                    j = 2 * pair + s
                    for k_pass in range(IN_PASSES):
                        feats = slice(k_pass * CHUNK + j * P, k_pass * CHUNK + (j + 1) * P)
                        toks = slice(k_pass * TOKENS, (k_pass + 1) * TOKENS)
                        mx_pass(
                            bank[:, s * TOKENS : (s + 1) * TOKENS],
                            win_codes[:, r, feats],
                            win_scales[:, r, feats],
                            x_codes[:, toks],
                            x_scales[:, toks],
                            k_pass == 0,
                            k_pass == IN_PASSES - 1,
                        )
                for s in range(2):
                    j = 2 * pair + s
                    nc.scalar.activation(
                        out=y_lin[:, j, :],
                        in_=bank[:, s * TOKENS : (s + 1) * TOKENS],
                        func=ACT.Copy,
                        scale=gain[:, 4 * r + j : 4 * r + j + 1],
                    )
            nc.gpsimd.tensor_scalar(
                out=y_grouped[:, r * 4 * TOKENS : (r + 1) * 4 * TOKENS].rearrange(
                    "p (t j) -> p t j", j=4
                ),
                in0=y_lin[:].rearrange("p j t -> p t j"),
                scalar1=1.0,
                scalar2=0.0,
                op0=ALU.mult,
                op1=ALU.add,
            )

        def second_matmul():
            for t in range(TOKEN_TILES):
                for half in range(2):
                    acc = work_banks.tile([P, BANK], F32, tag="bank")
                    for s in range(2):
                        chunk = 2 * half + s
                        for k_pass in range(OUT_PASSES):
                            toks = slice(k_pass * TOKENS + t * P, k_pass * TOKENS + (t + 1) * P)
                            cols = slice(k_pass * OUT_COLS, (k_pass + 1) * OUT_COLS)
                            mx_pass(
                                acc[:, s * OUT_COLS : (s + 1) * OUT_COLS],
                                y_codes[:, toks],
                                y_scales[:, toks],
                                wout_codes[:, chunk, cols],
                                wout_scales[:, chunk, cols],
                                k_pass == 0,
                                k_pass == OUT_PASSES - 1,
                            )
                    acc_of[(t, half)] = acc

        def one_over_rms():
            for t in range(TOKEN_TILES):
                mean_sq = small.tile([P, 2], F32, tag="mean_sq")
                rest = small.tile([P, 1], F32, tag="rest")
                rstd = small.tile([P, 1], F32, tag="rstd")
                for half in range(2):
                    unused = (2 * t + half) * BANK
                    nc.scalar.activation(
                        out=y_grouped[:, unused : unused + BANK],
                        in_=acc_of[(t, half)][:],
                        func=ACT.Square,
                        scale=D_MODEL**-0.5,
                        accum_out=mean_sq[:, half : half + 1],
                    )
                nc.scalar.activation(
                    out=rest[:], in_=mean_sq[:, 1:2], func=ACT.Identity, bias=eps_column[:, 0:1]
                )
                nc.scalar.activation(
                    out=rstd[:],
                    in_=mean_sq[:, 0:1],
                    func=ACT.Abs_reciprocal_sqrt,
                    bias=rest[:, 0:1],
                )
                rstd_of[t] = rstd

        def finish_rows(t):
            final = staging.tile([P, 2 * D_MODEL], F32, tag="stage")
            norm_w_values = norm_w_all[:].bitcast(BF16)
            for half in range(2):
                cols = slice(half * BANK, (half + 1) * BANK)
                nc.vector.scalar_tensor_tensor(
                    out=final[:, cols],
                    in0=acc_of[(t, half)][:],
                    scalar=rstd_of[t][:, 0:1],
                    in1=norm_w_values[:, cols],
                    op0=ALU.mult,
                    op1=ALU.mult,
                )
            nc.vector.tensor_tensor(
                out=final[:, D_MODEL : 2 * D_MODEL],
                in0=final[:, 0:D_MODEL],
                in1=x_sb[:, t * D_MODEL : (t + 1) * D_MODEL],
                op=ALU.add,
            )
            nc.scalar.dma_start(
                out=res_rows[t * P : (t + 1) * P, :], in_=final[:, D_MODEL : 2 * D_MODEL]
            )

        def after_quantise(n):
            if n + AHEAD < WEIGHT_CHUNKS:
                prepare_weights(n + AHEAD, [nc.scalar.copy])
            if n < ROUNDS:
                y_of_round(n)

        make_identity(nc, ident[:])
        nc.gpsimd.memset(gain_pad[:], 0.0)
        nc.gpsimd.memset(one[:], 1.0)
        nc.gpsimd.memset(eps_column[:], EPS)
        nc.vector.memset(table[NORM_W_ROW:P, :], 0.0)

        for part in range(2):
            nc.sync.dma_start(
                out=table[part * TABLE_ROWS : (part + 1) * TABLE_ROWS, :],
                in_=b_flat[part].rearrange("(r w) -> r w", w=TABLE_ROW),
            )
        nc.sync.dma_start(
            out=table[NORM_W_ROW : NORM_W_ROW + 4, :],
            in_=norm_w.rearrange("(r w) -> r w", w=TABLE_ROW),
        )
        nc.sync.dma_start(
            out=x_sb[:].rearrange("p (t k) -> p t k", t=TOKEN_TILES),
            in_=x_rows.rearrange("(t p) k -> p t k", p=P),
        )
        for n in range(RESIDENT):
            load_weights(n)

        gain_in_rows()

        nc.scalar.activation(out=warm[:], in_=one[:], func=ACT.Abs_reciprocal_sqrt)

        both = [nc.scalar.copy, nc.vector.tensor_copy]
        bank = work_banks.tile([P, BANK], F32, tag="bank")
        nc.tensor.transpose(out=bank[:, 0:P], in_=table[:].bitcast(F32), identity=ident[:])
        nc.vector.tensor_copy(out=table_columns[:], in_=bank[:, 0:P])
        x_grouped = grouping.tile([P, CHUNK_WORDS, 2], F32, tag="grouped", align_bytes=64)
        x_columns = IN_PASSES * TOKENS
        k_to_partitions(x_sb[:], TOKEN_TILES, IN_PASSES, x_grouped, both)
        nc.vector.quantize_mx(
            out=x_codes[:].bitcast(FP8X4),
            scales=x_scales[:],
            in_=x_grouped[:, 0:x_columns, :].rearrange("p c h -> p (c h)").bitcast(BF16),
        )
        prepare_weights(0, both)
        spread_b(0, nc.scalar.copy)
        quantise(0)
        xi_by_token(0)
        for n in range(1, AHEAD + 1):
            prepare_weights(n, [nc.scalar.copy])
        gain_to_partitions()
        y_of_round(0)
        grouped_of[Y_OPERAND] = y_grouped[:]

        for r in range(ROUNDS):
            for i in range(len(tiles_of_round)):
                t, part = tiles_of_round[i]
                state_products(r, t, part)
                done = r * len(tiles_of_round) + i + 1
                if done <= EARLY_CHUNKS:
                    n = done
                elif done % 2 == 0:
                    n = EARLY_CHUNKS + (done - EARLY_CHUNKS) // 2
                else:
                    n = WEIGHT_CHUNKS
                if n < WEIGHT_CHUNKS:
                    quantise(n)
                if n == 1:
                    xi_by_token(1)
                    spread_b(1, nc.scalar.copy)
                if n < WEIGHT_CHUNKS:
                    after_quantise(n)
                if n == WEIGHT_CHUNKS - AHEAD:
                    spread_b(2, nc.scalar.copy)
                    gpsimd_share(2)
                    spread_b(3, nc.scalar.copy)
                    spread_table_rows(NORM_W_ROW, norm_w_all[:], nc.scalar.copy)
                if r == 2 and i == 0:
                    gpsimd_share(3)
                if n == WEIGHT_CHUNKS - 1:
                    quantise(Y_OPERAND)
                    second_matmul()
                    one_over_rms()
            if r + 2 < ROUNDS:
                xi_by_token(r + 2)
                xi_for_gpsimd(r + 2)
        for t in range(TOKEN_TILES):
            finish_rows(t)
